import numpy as np
import ml_dtypes


def mxq(x, axis, fmt="e4m3"):
    dtype, down = {"e4m3": (ml_dtypes.float8_e4m3fn, 7), "e5m2": (ml_dtypes.float8_e5m2, 14)}[fmt]
    v = np.moveaxis(np.asarray(x, np.float32).astype(ml_dtypes.bfloat16).astype(np.float64), axis, -1)
    blocks = v.reshape(v.shape[:-1] + (-1, 32))
    amax = np.abs(blocks).max(-1, keepdims=True)
    byte = np.maximum(np.where(amax > 0, np.frexp(amax)[1] - 1 + 127, 0) - down, 1)
    scale = np.exp2(byte - 127.0)
    codes = (blocks / scale).astype(np.float32).astype(dtype).astype(np.float64)
    return np.moveaxis((codes * scale).reshape(v.shape), -1, axis)


WIDE = False


def mx_kscale(k):
    if not WIDE:
        return np.ones(k)
    levels = np.array([30, -30])
    if k % 512:
        return np.exp2(np.random.permutation(np.resize(levels, k // 32))).repeat(32)
    a = np.empty((k // 512, 16))
    for p in range(k // 512):
        a[p, :8] = np.random.permutation(np.resize(levels, 8))
        for g in range(8):
            far = levels[np.abs(levels - a[p, g]) >= 10]
            a[p, g + 8] = far[np.random.randint(len(far))]
    return np.exp2(a.ravel()).repeat(32)


BF16 = ml_dtypes.bfloat16


def bf(x):
    return np.asarray(x, np.float32).astype(BF16)


def f64(x):
    return np.asarray(x).astype(np.float64)


E2M1 = np.array([0.0, 0.5, 1.0, 1.5, 2.0, 3.0, 4.0, 6.0, -0.0, -0.5, -1.0, -1.5, -2.0, -3.0, -4.0, -6.0])


def pack_weight(w, fmt):
    k, n = w.shape
    w = f64(bf(w)).reshape(k // 32, 32, n)
    amax = np.abs(w).max(1)
    if fmt == "e4m3":
        byte = np.frexp(amax)[1] - 1 + 127 - 7
    else:
        mant, ex = np.frexp(amax / 6.0)
        byte = np.where(mant > 0.5, ex, ex - 1) + 127
    byte = np.clip(np.where(amax > 0, byte, 1), 1, 254)
    scaled = (w * np.exp2(127.0 - byte)[:, None, :]).reshape(k, n).astype(np.float32)
    by_word = np.ascontiguousarray(scaled.reshape(k // 512, 128, 4, n).transpose(0, 1, 3, 2))
    if fmt == "e4m3":
        words = by_word.astype(ml_dtypes.float8_e4m3fn).view(np.uint8)
    else:
        c = by_word.astype(ml_dtypes.float4_e2m1fn).view(np.uint8) & 0xF
        words = c[..., 0::2] | (c[..., 1::2] << 4)
    return np.ascontiguousarray(words), np.ascontiguousarray(byte.astype(np.uint8).reshape(k // 512, 16, n))


def unpack_weight(words, scales, fmt):
    g, p, n, _ = words.shape
    if fmt == "e4m3":
        vals = np.ascontiguousarray(words).view(ml_dtypes.float8_e4m3fn).astype(np.float64)
    else:
        nib = np.empty((g, p, n, 4), np.uint8)
        nib[..., 0::2] = words & 0xF
        nib[..., 1::2] = words >> 4
        vals = E2M1[nib]
    vals = vals * np.repeat(np.exp2(scales.astype(np.float64) - 127.0), 8, axis=1)[..., None]
    return vals.transpose(0, 1, 3, 2).reshape(g * 512, n)

def pack4(w):
    words, scales = pack_weight(w, "e2m1")
    return words.reshape(words.shape[0], 128, -1), scales


def unpack4(words, scales):
    return unpack_weight(words.reshape(words.shape[0], 128, -1, 2), scales, "e2m1")


B, F, H, C = 1024, 1024, 512, 10
EPS = 4.0 / 30.0
P_KEEP = 0.95


def setup_inputs():
    s = mx_kscale(F)
    ns = EPS / (6.0 * np.sqrt(H))
    x1 = bf(np.random.standard_normal((B, F)) * s)
    x2 = bf(np.random.standard_normal((B, F)) * s)
    W1_words, W1_scales = pack4(np.random.standard_normal((F, H)) / np.sqrt(F) / s[:, None])
    b1 = bf(np.random.standard_normal(H) * 0.3)
    W2_words, W2_scales = pack4(np.random.standard_normal((F, H)) / np.sqrt(F) / s[:, None])
    b2 = bf(np.random.standard_normal(H) * 0.3)
    noise_std = bf(np.random.laplace(size=(B, H)) * ns)
    rr_uniform = bf(np.random.uniform(size=H))
    return {"x1": x1,
            "x2": x2,
            "W1_words": W1_words,
            "W1_scales": W1_scales,
            "b1": b1,
            "W2_words": W2_words,
            "W2_scales": W2_scales,
            "b2": b2,
            "noise_std": noise_std,
            "rr_uniform": rr_uniform}


def reference(x1, x2, W1_words, W1_scales, b1, W2_words, W2_scales, b2, noise_std, rr_uniform):
    out1 = (mxq(f64(x1), 1, "e5m2") @ unpack4(W1_words, W1_scales)) + f64(b1)
    one_norm = np.sum(np.abs(out1), axis=1)
    sensitivity = np.max(one_norm) - np.min(one_norm)
    noise_mul = sensitivity / EPS
    out1 = out1 + f64(noise_std) * noise_mul
    rr_mask = np.where(f64(rr_uniform) < P_KEEP, 1.0, 0.0)
    out1 = out1 * rr_mask
    out2 = (mxq(f64(x2), 1, "e5m2") @ unpack4(W2_words, W2_scales)) + f64(b2)
    return np.minimum(out1, out2)

@@ -1,0 +1,345 @@
+from contextlib import ExitStack
+
+import concourse.mybir as mybir
+from concourse.masks import make_identity
+
+B, F, H = 1024, 1024, 512
+NOISE_GAIN = 30.0 / 4.0
+P_KEEP = 0.95
+FLOPS = 2 * 2 * B * F * H
+
+F32 = mybir.dt.float32
+BF16 = mybir.dt.bfloat16
+I32 = mybir.dt.int32
+U32 = mybir.dt.uint32
+U8 = mybir.dt.uint8
+E5M2 = mybir.dt.float8_e5m2_x4
+E2M1 = mybir.dt.float4_e2m1fn_x4
+ALU = mybir.AluOpType
+ACT = mybir.ActivationFunctionType
+AXIS = mybir.AxisListType
+
+P = 128
+TILES = B // P
+PAIRS = TILES // 2
+PASSES = F // 512
+H_TILES = H // P
+BANKS = 8
+EARLY_MASKED = 4
+
+
+def tile_splitnn_pa_kernel(
+    tc, x1, x2, W1_words, W1_scales, b1, W2_words, W2_scales, b2, noise_std, rr_uniform, out
+):
+    nc = tc.nc
+    x1_rows = x1.rearrange("(p t) k -> p t k", t=TILES)
+    x2_rows = x2.rearrange("(p t) k -> p t k", t=TILES)
+    noise_rows = noise_std.rearrange("(p t) h -> p t h", t=TILES)
+    out_rows = out.rearrange("(p t) h -> p t h", t=TILES)
+
+    with ExitStack() as ctx:
+        sb = ctx.enter_context(tc.tile_pool(name="sb", bufs=1))
+        psum = ctx.enter_context(tc.psum_pool(name="psum", bufs=1))
+        ctx.enter_context(tc.manual_schedule())
+
+        banks_taken = []
+
+        def next_bank():
+            tag = "bank%d" % (len(banks_taken) % BANKS)
+            banks_taken.append(tag)
+            bank = psum.tile([P, 512], F32, name=tag, tag=tag)
+            return bank
+
+        def keep_tile(name, shape, dtype):
+            kept = sb.tile(shape, dtype, name=name, tag=name, align_bytes=64)
+            return kept
+
+        ident = keep_tile("ident", [P, P], F32)
+        pick = keep_tile("pick", [P, H_TILES], BF16)
+        vec_rows = keep_tile("vec_rows", [P, H], BF16)
+        b2_rows = keep_tile("b2_rows", [P, P], BF16)
+        b1_all = keep_tile("b1_all", [P, H], F32)
+        keep_all = keep_tile("keep_all", [P, H], BF16)
+        b2_cols = keep_tile("b2_cols", [P, H_TILES], F32)
+        w_words = [keep_tile("w_words%d" % c, [P, PASSES, 2 * H], U8) for c in range(2)]
+        w_plane = [keep_tile("w_plane%d" % c, [P, PASSES, H], U8) for c in range(2)]
+        x1_sb = [keep_tile("x1_sb%d" % j, [P, 2, F], BF16) for j in range(PAIRS)]
+        x2_sb = [keep_tile("x2_sb%d" % j, [P, 2, F], BF16) for j in range(PAIRS)]
+        noise_sb = [keep_tile("noise_sb%d" % j, [P, TILES // 2, H], BF16) for j in range(2)]
+        norms = keep_tile("norms", [P, TILES], F32)
+        extremes = keep_tile("extremes", [P, 2], F32)
+        lowest = keep_tile("lowest", [P, 1], F32)
+        noise_mul = keep_tile("noise_mul", [P, 1], F32)
+        a_sb = [keep_tile("a_sb%d" % t, [P, H], F32) for t in range(TILES)]
+        am_sb = [keep_tile("am_sb%d" % t, [P, H], F32) for t in range(EARLY_MASKED)]
+        nm_sb = [keep_tile("nm_sb%d" % t, [P, H], BF16) for t in range(EARLY_MASKED)]
+        c_sb = [keep_tile("c_sb%d" % t, [P, H], F32) for t in range(TILES)]
+        cm_sb = dict((t, keep_tile("cm_sb%d" % t, [P, H], F32)) for t in range(EARLY_MASKED, TILES))
+        out_sb = [keep_tile("out_sb%d" % t, [P, H], F32) for t in range(TILES)]
+        dT_sb = [keep_tile("dT_sb%d" % j, [P, H_TILES, 2 * P], F32) for j in range(PAIRS)]
+
+        def load_weights(c, words, scales):
+            nc.sync.dma_start(
+                out=w_words[c][:].bitcast(I32), in_=words.rearrange("g p n -> p g n").bitcast(I32)
+            )
+            for q in range(4):
+                nc.sync.dma_start(
+                    out=w_plane[c][32 * q : 32 * q + 4, :, :].bitcast(I32),
+                    in_=scales[:, 4 * q : 4 * q + 4, :].rearrange("g r n -> r g n").bitcast(I32),
+                )
+
+        make_identity(nc, ident[:])
+        nc.vector.memset(vec_rows[:], 0.0)
+        nc.vector.memset(w_plane[0][:].bitcast(I32), 0)
+        nc.vector.memset(b2_rows[:], 0.0)
+        nc.vector.memset(w_plane[1][:].bitcast(I32), 0)
+        nc.vector.tensor_copy(out=pick[:], in_=ident[:, 0:H_TILES])
+
+        nc.sync.dma_start(out=x1_sb[0][:, 0, :], in_=x1_rows[:, 0, :])
+        nc.sync.dma_start(out=vec_rows[0:1, :], in_=b1.rearrange("(o n) -> o n", o=1))
+        nc.sync.dma_start(out=vec_rows[1:2, :], in_=rr_uniform.rearrange("(o n) -> o n", o=1))
+        nc.sync.dma_start(out=x1_sb[0][:, 1, :], in_=x1_rows[:, 1, :])
+        nc.sync.dma_start(out=x1_sb[1][:], in_=x1_rows[:, 2:4, :])
+        load_weights(0, W1_words, W1_scales)
+        nc.sync.dma_start(out=x1_sb[2][:], in_=x1_rows[:, 4:6, :])
+        nc.sync.dma_start(out=x1_sb[3][:], in_=x1_rows[:, 6:8, :])
+        nc.sync.dma_start(out=b2_rows[0:H_TILES, :], in_=b2.rearrange("(c p) -> c p", p=P))
+        nc.sync.dma_start(out=noise_sb[0][:], in_=noise_rows[:, 0:4, :])
+        nc.sync.dma_start(out=x2_sb[0][:], in_=x2_rows[:, 0:2, :])
+        load_weights(1, W2_words, W2_scales)
+        nc.sync.dma_start(out=x2_sb[1][:], in_=x2_rows[:, 2:4, :])
+        nc.sync.dma_start(out=x2_sb[2][:], in_=x2_rows[:, 4:6, :])
+        nc.sync.dma_start(out=noise_sb[1][:], in_=noise_rows[:, 4:8, :])
+        nc.sync.dma_start(out=x2_sb[3][:], in_=x2_rows[:, 6:8, :])
+
+        b1_bank = next_bank()
+        nc.tensor.matmul(b1_bank[:], lhsT=pick[:, 0:1].to_broadcast([P, P]), rhs=vec_rows[:], start=True, stop=True)
+        rr_bank = next_bank()
+        nc.tensor.matmul(rr_bank[:], lhsT=pick[:, 1:2].to_broadcast([P, P]), rhs=vec_rows[:], start=True, stop=True)
+        nc.scalar.activation(out=b1_all[:], in_=b1_bank[:], func=ACT.Identity)
+        nc.vector.tensor_scalar(
+            out=keep_all[:], in0=rr_bank[:], scalar1=P_KEEP, scalar2=None, op0=ALU.is_lt
+        )
+
+        turned = {}
+        grouped = {}
+        codes = {}
+        scales = {}
+
+        def turn(key, sources):
+            bank = next_bank()
+            for s, (rows, g) in enumerate(sources):
+                words = rows.bitcast(F32)
+                for u in range(2):
+                    nc.tensor.transpose(
+                        bank[:, P * (2 * s + u) : P * (2 * s + u + 1)],
+                        words[:, 256 * g + u : 256 * (g + 1) : 2],
+                        ident[:],
+                    )
+            turned[key] = bank
+
+        def interleave(key):
+            staged = sb.tile([P, 1024], BF16, name="staged", tag="staged", bufs=6, align_bytes=64)
+            nc.scalar.copy(
+                out=staged[:].bitcast(F32).rearrange("p (s r u) -> p s r u", s=2, u=2),
+                in_=turned[key][:].rearrange("p (s u r) -> p s r u", s=2, u=2),
+            )
+            grouped[key] = staged
+
+        def quantize(key):
+            words = sb.tile([P, 256], U32, name="codes", tag="codes", bufs=16, align_bytes=64)
+            plane = sb.tile([P, 256], U8, name="plane", tag="plane", bufs=16, align_bytes=64)
+            nc.vector.quantize_mx(out=words[:].bitcast(E5M2), scales=plane[:], in_=grouped[key][:])
+            codes[key] = words
+            scales[key] = plane
+
+        def turn_x1(t):
+            turn(("x1", t), [(x1_sb[t // 2][:, t % 2, :], g) for g in range(PASSES)])
+            interleave(("x1", t))
+
+        def turn_x2(j, g):
+            turn(("x2", j, g), [(x2_sb[j][:, s, :], g) for s in range(2)])
+            interleave(("x2", j, g))
+
+        p1 = {}
+
+        def product1(t):
+            bank = next_bank()
+            for g in range(PASSES):
+                cols = slice(P * g, P * (g + 1))
+                nc.tensor.matmul_mx(
+                    out=bank[:],
+                    lhsT=codes[("x1", t)][:, cols].bitcast(E5M2),
+                    lhsT_scale=scales[("x1", t)][:, cols],
+                    rhs=w_words[0][:, g, :].bitcast(E2M1),
+                    rhs_scale=w_plane[0][:, g, :],
+                    start=(g == 0),
+                    stop=(g == PASSES - 1),
+                )
+            p1[t] = bank
+
+        def add_b1(t):
+            nc.vector.tensor_tensor(out=a_sb[t][:], in0=p1[t][:], in1=b1_all[:], op=ALU.add)
+
+        def row_norm(t):
+            magnitudes = sb.tile([P, H], BF16, name="magnitudes", tag="magnitudes", bufs=2)
+            nc.scalar.activation(
+                out=magnitudes[:], in_=a_sb[t][:], func=ACT.Abs, scale=NOISE_GAIN, accum_out=norms[:, t : t + 1]
+            )
+
+        def mask_a(t):
+            nc.vector.tensor_tensor(out=am_sb[t][:], in0=a_sb[t][:], in1=keep_all[:], op=ALU.mult)
+
+        def mask_noise(t):
+            nc.vector.tensor_tensor(out=nm_sb[t][:], in0=noise_sb[0][:, t, :], in1=keep_all[:], op=ALU.mult)
+
+        def product2(j):
+            for half in range(2):
+                bank = next_bank()
+                for i in range(2):
+                    h = 2 * half + i
+                    for g in range(PASSES):
+                        nc.tensor.matmul_mx(
+                            out=bank[:, 256 * i : 256 * (i + 1)],
+                            lhsT=w_words[1][:, g, 2 * P * h : 2 * P * (h + 1)].bitcast(E2M1),
+                            lhsT_scale=w_plane[1][:, g, P * h : P * (h + 1)],
+                            rhs=codes[("x2", j, g)][:].bitcast(E5M2),
+                            rhs_scale=scales[("x2", j, g)][:],
+                            start=(g == 0),
+                            stop=(g == PASSES - 1),
+                        )
+                for i in range(2):
+                    h = 2 * half + i
+                    nc.scalar.activation(
+                        out=dT_sb[j][:, h, :],
+                        in_=bank[:, 256 * i : 256 * (i + 1)],
+                        func=ACT.Identity,
+                        bias=b2_cols[:, h : h + 1],
+                    )
+
+        d_bank = {}
+
+        def turn_back(j):
+            for s in range(2):
+                bank = next_bank()
+                for h in range(H_TILES):
+                    nc.tensor.transpose(bank[:, P * h : P * (h + 1)], dT_sb[j][:, h, P * s : P * (s + 1)], ident[:])
+                d_bank[2 * j + s] = bank
+
+        def add_noise(t):
+            if t < EARLY_MASKED:
+                noise, a = nm_sb[t][:], am_sb[t][:]
+            else:
+                noise, a = noise_sb[1][:, t - TILES // 2, :], a_sb[t][:]
+            nc.vector.scalar_tensor_tensor(
+                out=c_sb[t][:], in0=noise, scalar=noise_mul[:, 0:1], in1=a, op0=ALU.mult, op1=ALU.add
+            )
+
+        def mask_c(t):
+            nc.vector.tensor_tensor(out=cm_sb[t][:], in0=c_sb[t][:], in1=keep_all[:], op=ALU.mult)
+
+        def finish(t):
+            c = c_sb[t] if t < EARLY_MASKED else cm_sb[t]
+            nc.vector.tensor_tensor(out=out_sb[t][:], in0=c[:], in1=d_bank[t][:], op=ALU.min)
+            nc.sync.dma_start(out=out_rows[:, t, :], in_=out_sb[t][:])
+
+        for t in range(4):
+            turn_x1(t)
+            quantize(("x1", t))
+        product1(0)
+        product1(1)
+        add_b1(0)
+        add_b1(1)
+        row_norm(0)
+        mask_a(0)
+        turn_x1(4)
+        quantize(("x1", 4))
+        mask_a(1)
+        turn_x1(5)
+        quantize(("x1", 5))
+        row_norm(1)
+        product1(2)
+        product1(3)
+        add_b1(2)
+        add_b1(3)
+        row_norm(2)
+        turn_x1(6)
+        quantize(("x1", 6))
+        mask_noise(0)
+        turn_x1(7)
+        quantize(("x1", 7))
+        row_norm(3)
+        b2_bank = next_bank()
+        nc.tensor.matmul(b2_bank[:, 0:H_TILES], lhsT=b2_rows[:], rhs=pick[:], start=True, stop=True)
+        nc.scalar.copy(out=b2_cols[:], in_=b2_bank[:, 0:H_TILES])
+        for t in range(4, 8):
+            product1(t)
+            add_b1(t)
+            row_norm(t)
+        mask_a(2)
+
+        nc.vector.tensor_reduce(out=extremes[:, 0:1], in_=norms[:], axis=AXIS.X, op=ALU.min)
+        nc.vector.tensor_reduce(out=extremes[:, 1:2], in_=norms[:], axis=AXIS.X, op=ALU.max)
+        turn_x2(0, 0)
+        turn_x2(0, 1)
+        quantize(("x2", 0, 0))
+        mask_noise(1)
+        quantize(("x2", 0, 1))
+        turn_x2(1, 0)
+        turn_x2(1, 1)
+        ends_bank = next_bank()
+        for e in range(2):
+            nc.tensor.transpose(
+                ends_bank[:, P * e : P * (e + 1)], extremes[:, e : e + 1].to_broadcast([P, P]), ident[:]
+            )
+        mask_a(3)
+        nc.vector.tensor_reduce(out=lowest[:], in_=ends_bank[:, 0:P], axis=AXIS.X, op=ALU.min)
+        mask_noise(2)
+        spans = keep_tile("spans", [P, P], F32)
+        nc.vector.tensor_scalar(
+            out=spans[:],
+            in0=ends_bank[:, P : 2 * P],
+            scalar1=lowest[:, 0:1],
+            scalar2=None,
+            op0=ALU.subtract,
+            op1=ALU.max,
+            accum_out=noise_mul[:],
+        )
+        quantize(("x2", 1, 0))
+        mask_noise(3)
+        quantize(("x2", 1, 1))
+
+        product2(0)
+        for t in range(4):
+            add_noise(t)
+        turn_x2(2, 0)
+        turn_x2(2, 1)
+        turn_back(0)
+        product2(1)
+        quantize(("x2", 2, 0))
+        quantize(("x2", 2, 1))
+        finish(0)
+        add_noise(4)
+        finish(1)
+        mask_c(4)
+        turn_x2(3, 0)
+        turn_x2(3, 1)
+        turn_back(1)
+        product2(2)
+        add_noise(5)
+        quantize(("x2", 3, 0))
+        mask_c(5)
+        quantize(("x2", 3, 1))
+        product2(3)
+        turn_back(2)
+        add_noise(6)
+        finish(2)
+        mask_c(6)
+        finish(3)
+        turn_back(3)
+        add_noise(7)
+        finish(4)
+        mask_c(7)
+        finish(5)
+        finish(6)
+        finish(7)

@@ -22,10 +22,14 @@ AXIS = mybir.AxisListType
 P = 128
 TILES = B // P
 PAIRS = TILES // 2
+PAIR_ROWS = 2 * P
 PASSES = F // 512
+PASS_WORDS = 256
 H_TILES = H // P
 BANKS = 8
-EARLY_MASKED = 4
+BANK_COLS = 512
+OPERANDS = 2 * TILES
+STAGED_BUFS = 6
 
 
 def tile_splitnn_pa_kernel(
@@ -47,84 +51,98 @@ def tile_splitnn_pa_kernel(
         def next_bank():
             tag = "bank%d" % (len(banks_taken) % BANKS)
             banks_taken.append(tag)
-            bank = psum.tile([P, 512], F32, name=tag, tag=tag)
+            bank = psum.tile([P, BANK_COLS], F32, name=tag, tag=tag)
             return bank
 
-        def keep_tile(name, shape, dtype):
-            kept = sb.tile(shape, dtype, name=name, tag=name, align_bytes=64)
-            return kept
+        def resident(name, shape, dtype):
+            tile = sb.tile(shape, dtype, name=name, tag=name, align_bytes=64)
+            return tile
 
-        ident = keep_tile("ident", [P, P], F32)
-        pick = keep_tile("pick", [P, H_TILES], BF16)
-        vec_rows = keep_tile("vec_rows", [P, H], BF16)
-        b2_rows = keep_tile("b2_rows", [P, P], BF16)
-        b1_all = keep_tile("b1_all", [P, H], F32)
-        keep_all = keep_tile("keep_all", [P, H], BF16)
-        b2_cols = keep_tile("b2_cols", [P, H_TILES], F32)
-        w_words = [keep_tile("w_words%d" % c, [P, PASSES, 2 * H], U8) for c in range(2)]
-        w_plane = [keep_tile("w_plane%d" % c, [P, PASSES, H], U8) for c in range(2)]
-        x1_sb = [keep_tile("x1_sb%d" % j, [P, 2, F], BF16) for j in range(PAIRS)]
-        x2_sb = [keep_tile("x2_sb%d" % j, [P, 2, F], BF16) for j in range(PAIRS)]
-        noise_sb = [keep_tile("noise_sb%d" % j, [P, TILES // 2, H], BF16) for j in range(2)]
-        norms = keep_tile("norms", [P, TILES], F32)
-        extremes = keep_tile("extremes", [P, 2], F32)
-        lowest = keep_tile("lowest", [P, 1], F32)
-        noise_mul = keep_tile("noise_mul", [P, 1], F32)
-        a_sb = [keep_tile("a_sb%d" % t, [P, H], F32) for t in range(TILES)]
-        am_sb = [keep_tile("am_sb%d" % t, [P, H], F32) for t in range(EARLY_MASKED)]
-        nm_sb = [keep_tile("nm_sb%d" % t, [P, H], BF16) for t in range(EARLY_MASKED)]
-        c_sb = [keep_tile("c_sb%d" % t, [P, H], F32) for t in range(TILES)]
-        cm_sb = dict((t, keep_tile("cm_sb%d" % t, [P, H], F32)) for t in range(EARLY_MASKED, TILES))
-        out_sb = [keep_tile("out_sb%d" % t, [P, H], F32) for t in range(TILES)]
-        dT_sb = [keep_tile("dT_sb%d" % j, [P, H_TILES, 2 * P], F32) for j in range(PAIRS)]
+        ident = resident("ident", [P, P], F32)
+        pick = resident("pick", [P, 2 * H_TILES], BF16)
+        b1_row = resident("b1_row", [P, H], BF16)
+        rr_row = resident("rr_row", [P, H], BF16)
+        col_rows = resident("col_rows", [P, P], BF16)
+        b1_all = resident("b1_all", [P, H], F32)
+        keep_all = resident("keep_all", [P, H], BF16)
+        b2_cols = resident("b2_cols", [P, H_TILES], F32)
+        keep_cols = resident("keep_cols", [P, H_TILES], F32)
+        w_words = [resident("w_words%d" % c, [P, PASSES, 2 * H], U8) for c in range(2)]
+        w_scales = [resident("w_scales%d" % c, [P, PASSES, H], U8) for c in range(2)]
+        x1_sb = [resident("x1_sb%d" % j, [P, 2, F], BF16) for j in range(PAIRS)]
+        x2_sb = [resident("x2_sb%d" % j, [P, 2, F], BF16) for j in range(PAIRS)]
+        noise_sb = [resident("noise_sb%d" % j, [P, 2, H], BF16) for j in range(PAIRS)]
+        norms = resident("norms", [P, TILES], F32)
+        extremes = resident("extremes", [P, 2], F32)
+        lowest = resident("lowest", [P, 1], F32)
+        noise_mul = resident("noise_mul", [P, 1], F32)
+        a_sb = [resident("a_sb%d" % t, [P, H], F32) for t in range(TILES)]
+        a_kept = [resident("a_kept%d" % t, [P, H], F32) for t in range(2)]
+        noise_kept = [resident("noise_kept%d" % t, [P, H], BF16) for t in range(2)]
+        c_sb = [resident("c_sb%d" % t, [P, H], F32) for t in range(TILES)]
+        dT_sb = [resident("dT_sb%d" % j, [P, H_TILES, PAIR_ROWS], F32) for j in range(PAIRS)]
+        outT_sb = dict((j, resident("outT_sb%d" % j, [P, H_TILES, PAIR_ROWS], F32)) for j in range(1, PAIRS))
+        out_sb = [resident("out_sb%d" % t, [P, H], F32) for t in range(TILES)]
 
-        def load_weights(c, words, scales):
-            nc.sync.dma_start(
-                out=w_words[c][:].bitcast(I32), in_=words.rearrange("g p n -> p g n").bitcast(I32)
-            )
+        def pair(j):
+            return (2 * j, 2 * j + 1)
+
+
+        def load_pair(tiles, rows, j):
+            nc.sync.dma_start(out=tiles[j][:], in_=rows[:, 2 * j : 2 * j + 2, :])
+
+        def load_weights(c, words, scale_rows):
+            nc.sync.dma_start(out=w_words[c][:].bitcast(I32), in_=words.rearrange("g p n -> p g n").bitcast(I32))
             for q in range(4):
                 nc.sync.dma_start(
-                    out=w_plane[c][32 * q : 32 * q + 4, :, :].bitcast(I32),
-                    in_=scales[:, 4 * q : 4 * q + 4, :].rearrange("g r n -> r g n").bitcast(I32),
+                    out=w_scales[c][32 * q : 32 * q + 4, :, :].bitcast(I32),
+                    in_=scale_rows[:, 4 * q : 4 * q + 4, :].rearrange("g r n -> r g n").bitcast(I32),
                 )
 
         make_identity(nc, ident[:])
-        nc.vector.memset(vec_rows[:], 0.0)
-        nc.vector.memset(w_plane[0][:].bitcast(I32), 0)
-        nc.vector.memset(b2_rows[:], 0.0)
-        nc.vector.memset(w_plane[1][:].bitcast(I32), 0)
-        nc.vector.tensor_copy(out=pick[:], in_=ident[:, 0:H_TILES])
+        nc.vector.memset(b1_row[:], 0.0)
+        nc.vector.memset(w_scales[0][:].bitcast(I32), 0)
+        nc.vector.memset(rr_row[:], 0.0)
+        nc.vector.memset(col_rows[:], 0.0)
+        nc.vector.memset(w_scales[1][:].bitcast(I32), 0)
+        nc.scalar.activation(out=pick[:], in_=ident[:, 0 : 2 * H_TILES], func=ACT.Identity)
 
         nc.sync.dma_start(out=x1_sb[0][:, 0, :], in_=x1_rows[:, 0, :])
-        nc.sync.dma_start(out=vec_rows[0:1, :], in_=b1.rearrange("(o n) -> o n", o=1))
-        nc.sync.dma_start(out=vec_rows[1:2, :], in_=rr_uniform.rearrange("(o n) -> o n", o=1))
+        nc.sync.dma_start(out=b1_row[0:1, :], in_=b1.rearrange("(o n) -> o n", o=1))
+        nc.sync.dma_start(out=rr_row[0:1, :], in_=rr_uniform.rearrange("(o n) -> o n", o=1))
         nc.sync.dma_start(out=x1_sb[0][:, 1, :], in_=x1_rows[:, 1, :])
-        nc.sync.dma_start(out=x1_sb[1][:], in_=x1_rows[:, 2:4, :])
+        load_pair(x1_sb, x1_rows, 1)
         load_weights(0, W1_words, W1_scales)
-        nc.sync.dma_start(out=x1_sb[2][:], in_=x1_rows[:, 4:6, :])
-        nc.sync.dma_start(out=x1_sb[3][:], in_=x1_rows[:, 6:8, :])
-        nc.sync.dma_start(out=b2_rows[0:H_TILES, :], in_=b2.rearrange("(c p) -> c p", p=P))
-        nc.sync.dma_start(out=noise_sb[0][:], in_=noise_rows[:, 0:4, :])
-        nc.sync.dma_start(out=x2_sb[0][:], in_=x2_rows[:, 0:2, :])
+        load_pair(x1_sb, x1_rows, 2)
+        load_pair(noise_sb, noise_rows, 0)
+        load_pair(x1_sb, x1_rows, 3)
+        nc.sync.dma_start(out=col_rows[0:H_TILES, :], in_=b2.rearrange("(h p) -> h p", p=P))
+        nc.sync.dma_start(out=col_rows[H_TILES : 2 * H_TILES, :], in_=rr_uniform.rearrange("(h p) -> h p", p=P))
+        load_pair(x2_sb, x2_rows, 1)
         load_weights(1, W2_words, W2_scales)
-        nc.sync.dma_start(out=x2_sb[1][:], in_=x2_rows[:, 2:4, :])
-        nc.sync.dma_start(out=x2_sb[2][:], in_=x2_rows[:, 4:6, :])
-        nc.sync.dma_start(out=noise_sb[1][:], in_=noise_rows[:, 4:8, :])
-        nc.sync.dma_start(out=x2_sb[3][:], in_=x2_rows[:, 6:8, :])
+        load_pair(x2_sb, x2_rows, 2)
+        load_pair(noise_sb, noise_rows, 1)
+        load_pair(x2_sb, x2_rows, 3)
+        load_pair(noise_sb, noise_rows, 2)
+        load_pair(noise_sb, noise_rows, 3)
+        load_pair(x2_sb, x2_rows, 0)
 
-        b1_bank = next_bank()
-        nc.tensor.matmul(b1_bank[:], lhsT=pick[:, 0:1].to_broadcast([P, P]), rhs=vec_rows[:], start=True, stop=True)
-        rr_bank = next_bank()
-        nc.tensor.matmul(rr_bank[:], lhsT=pick[:, 1:2].to_broadcast([P, P]), rhs=vec_rows[:], start=True, stop=True)
-        nc.scalar.activation(out=b1_all[:], in_=b1_bank[:], func=ACT.Identity)
-        nc.vector.tensor_scalar(
-            out=keep_all[:], in0=rr_bank[:], scalar1=P_KEEP, scalar2=None, op0=ALU.is_lt
-        )
 
-        turned = {}
-        grouped = {}
-        codes = {}
-        scales = {}
+        def spread_row(row_tile):
+            bank = next_bank()
+            nc.tensor.matmul(bank[:], lhsT=pick[:, 0:1].to_broadcast([P, P]), rhs=row_tile[:], start=True, stop=True)
+            return bank
+
+        def is_kept(dst, uniform):
+            nc.vector.tensor_scalar(out=dst, in0=uniform, scalar1=P_KEEP, scalar2=None, op0=ALU.is_lt)
+
+        def turn_col_rows():
+            bank = next_bank()
+            nc.tensor.matmul(bank[:, 0 : 2 * H_TILES], lhsT=col_rows[:], rhs=pick[:], start=True, stop=True)
+            return bank
+
+
+        turned, staged, codes, scales = {}, {}, {}, {}
 
         def turn(key, sources):
             bank = next_bank()
@@ -133,35 +151,35 @@ def tile_splitnn_pa_kernel(
                 for u in range(2):
                     nc.tensor.transpose(
                         bank[:, P * (2 * s + u) : P * (2 * s + u + 1)],
-                        words[:, 256 * g + u : 256 * (g + 1) : 2],
+                        words[:, PASS_WORDS * g + u : PASS_WORDS * (g + 1) : 2],
                         ident[:],
                     )
             turned[key] = bank
 
-        def interleave(key):
-            staged = sb.tile([P, 1024], BF16, name="staged", tag="staged", bufs=6, align_bytes=64)
-            nc.scalar.copy(
-                out=staged[:].bitcast(F32).rearrange("p (s r u) -> p s r u", s=2, u=2),
-                in_=turned[key][:].rearrange("p (s u r) -> p s r u", s=2, u=2),
-            )
-            grouped[key] = staged
-
-        def quantize(key):
-            words = sb.tile([P, 256], U32, name="codes", tag="codes", bufs=16, align_bytes=64)
-            plane = sb.tile([P, 256], U8, name="plane", tag="plane", bufs=16, align_bytes=64)
-            nc.vector.quantize_mx(out=words[:].bitcast(E5M2), scales=plane[:], in_=grouped[key][:])
-            codes[key] = words
-            scales[key] = plane
-
         def turn_x1(t):
             turn(("x1", t), [(x1_sb[t // 2][:, t % 2, :], g) for g in range(PASSES)])
-            interleave(("x1", t))
 
-        def turn_x2(j, g):
-            turn(("x2", j, g), [(x2_sb[j][:, s, :], g) for s in range(2)])
-            interleave(("x2", j, g))
+        def turn_x2(j):
+            for g in range(PASSES):
+                turn(("x2", j, g), [(x2_sb[j][:, s, :], g) for s in range(2)])
 
-        p1 = {}
+        def interleave(key, copy=nc.scalar.copy):
+            tile = sb.tile([P, 2 * BANK_COLS], BF16, name="staged", tag="staged", bufs=STAGED_BUFS, align_bytes=64)
+            copy(
+                out=tile[:].bitcast(F32).rearrange("p (s r u) -> p s r u", s=2, u=2),
+                in_=turned[key][:].rearrange("p (s u r) -> p s r u", s=2, u=2),
+            )
+            staged[key] = tile
+
+        def quantize(key):
+            words = sb.tile([P, 2 * P], U32, name="codes", tag="codes", bufs=OPERANDS, align_bytes=64)
+            scale_bytes = sb.tile([P, 2 * P], U8, name="scales", tag="scales", bufs=OPERANDS, align_bytes=64)
+            nc.vector.quantize_mx(out=words[:].bitcast(E5M2), scales=scale_bytes[:], in_=staged[key][:])
+            codes[key] = words
+            scales[key] = scale_bytes
+
+
+        p1_bank = {}
 
         def product1(t):
             bank = next_bank()
@@ -172,14 +190,14 @@ def tile_splitnn_pa_kernel(
                     lhsT=codes[("x1", t)][:, cols].bitcast(E5M2),
                     lhsT_scale=scales[("x1", t)][:, cols],
                     rhs=w_words[0][:, g, :].bitcast(E2M1),
-                    rhs_scale=w_plane[0][:, g, :],
+                    rhs_scale=w_scales[0][:, g, :],
                     start=(g == 0),
                     stop=(g == PASSES - 1),
                 )
-            p1[t] = bank
+            p1_bank[t] = bank
 
         def add_b1(t):
-            nc.vector.tensor_tensor(out=a_sb[t][:], in0=p1[t][:], in1=b1_all[:], op=ALU.add)
+            nc.vector.tensor_tensor(out=a_sb[t][:], in0=p1_bank[t][:], in1=b1_all[:], op=ALU.add)
 
         def row_norm(t):
             magnitudes = sb.tile([P, H], BF16, name="magnitudes", tag="magnitudes", bufs=2)
@@ -188,116 +206,169 @@ def tile_splitnn_pa_kernel(
             )
 
         def mask_a(t):
-            nc.vector.tensor_tensor(out=am_sb[t][:], in0=a_sb[t][:], in1=keep_all[:], op=ALU.mult)
+            nc.vector.tensor_tensor(out=a_kept[t][:], in0=a_sb[t][:], in1=keep_all[:], op=ALU.mult)
 
         def mask_noise(t):
-            nc.vector.tensor_tensor(out=nm_sb[t][:], in0=noise_sb[0][:, t, :], in1=keep_all[:], op=ALU.mult)
+            nc.vector.tensor_tensor(out=noise_kept[t][:], in0=noise_sb[0][:, t, :], in1=keep_all[:], op=ALU.mult)
+
+        def add_noise(t):
+            if t in pair(0):
+                noise, a = noise_kept[t][:], a_kept[t][:]
+            else:
+                noise, a = noise_sb[t // 2][:, t % 2, :], a_sb[t][:]
+            nc.vector.scalar_tensor_tensor(
+                out=c_sb[t][:], in0=noise, scalar=noise_mul[:, 0:1], in1=a, op0=ALU.mult, op1=ALU.add
+            )
+
+
+        p2_bank, cT_bank, back_bank = {}, {}, {}
+
+        def half_cols(h):
+            return slice(PAIR_ROWS * (h % 2), PAIR_ROWS * (h % 2 + 1))
 
         def product2(j):
             for half in range(2):
                 bank = next_bank()
-                for i in range(2):
-                    h = 2 * half + i
+                for h in pair(half):
                     for g in range(PASSES):
                         nc.tensor.matmul_mx(
-                            out=bank[:, 256 * i : 256 * (i + 1)],
+                            out=bank[:, half_cols(h)],
                             lhsT=w_words[1][:, g, 2 * P * h : 2 * P * (h + 1)].bitcast(E2M1),
-                            lhsT_scale=w_plane[1][:, g, P * h : P * (h + 1)],
+                            lhsT_scale=w_scales[1][:, g, P * h : P * (h + 1)],
                             rhs=codes[("x2", j, g)][:].bitcast(E5M2),
                             rhs_scale=scales[("x2", j, g)][:],
                             start=(g == 0),
                             stop=(g == PASSES - 1),
                         )
-                for i in range(2):
-                    h = 2 * half + i
+                p2_bank[(j, half)] = bank
+
+        def add_b2(j, halves=(0, 1)):
+            for half in halves:
+                for h in pair(half):
                     nc.scalar.activation(
                         out=dT_sb[j][:, h, :],
-                        in_=bank[:, 256 * i : 256 * (i + 1)],
+                        in_=p2_bank[(j, half)][:, half_cols(h)],
                         func=ACT.Identity,
                         bias=b2_cols[:, h : h + 1],
                     )
 
-        d_bank = {}
+        def turn_c(j):
+            for half in range(2):
+                bank = next_bank()
+                for h in pair(half):
+                    for s in range(2):
+                        first = PAIR_ROWS * (h % 2) + P * s
+                        nc.tensor.transpose(
+                            bank[:, first : first + P], c_sb[2 * j + s][:, P * h : P * (h + 1)], ident[:]
+                        )
+                cT_bank[(j, half)] = bank
 
-        def turn_back(j):
+        def mask_and_min(j):
+            for h in range(H_TILES):
+                nc.vector.scalar_tensor_tensor(
+                    out=outT_sb[j][:, h, :],
+                    in0=cT_bank[(j, h // 2)][:, half_cols(h)],
+                    scalar=keep_cols[:, h : h + 1],
+                    in1=dT_sb[j][:, h, :],
+                    op0=ALU.mult,
+                    op1=ALU.min,
+                )
+
+        def turn_back(j, source):
             for s in range(2):
                 bank = next_bank()
                 for h in range(H_TILES):
-                    nc.tensor.transpose(bank[:, P * h : P * (h + 1)], dT_sb[j][:, h, P * s : P * (s + 1)], ident[:])
-                d_bank[2 * j + s] = bank
+                    nc.tensor.transpose(bank[:, P * h : P * (h + 1)], source[:, h, P * s : P * (s + 1)], ident[:])
+                back_bank[2 * j + s] = bank
 
-        def add_noise(t):
-            if t < EARLY_MASKED:
-                noise, a = nm_sb[t][:], am_sb[t][:]
-            else:
-                noise, a = noise_sb[1][:, t - TILES // 2, :], a_sb[t][:]
-            nc.vector.scalar_tensor_tensor(
-                out=c_sb[t][:], in0=noise, scalar=noise_mul[:, 0:1], in1=a, op0=ALU.mult, op1=ALU.add
-            )
-
-        def mask_c(t):
-            nc.vector.tensor_tensor(out=cm_sb[t][:], in0=c_sb[t][:], in1=keep_all[:], op=ALU.mult)
-
-        def finish(t):
-            c = c_sb[t] if t < EARLY_MASKED else cm_sb[t]
-            nc.vector.tensor_tensor(out=out_sb[t][:], in0=c[:], in1=d_bank[t][:], op=ALU.min)
+        def copy_and_store(t):
+            nc.scalar.copy(out=out_sb[t][:], in_=back_bank[t][:])
             nc.sync.dma_start(out=out_rows[:, t, :], in_=out_sb[t][:])
 
-        for t in range(4):
-            turn_x1(t)
-            quantize(("x1", t))
-        product1(0)
-        product1(1)
-        add_b1(0)
-        add_b1(1)
-        row_norm(0)
-        mask_a(0)
-        turn_x1(4)
-        quantize(("x1", 4))
-        mask_a(1)
-        turn_x1(5)
-        quantize(("x1", 5))
-        row_norm(1)
-        product1(2)
-        product1(3)
-        add_b1(2)
-        add_b1(3)
-        row_norm(2)
-        turn_x1(6)
-        quantize(("x1", 6))
-        mask_noise(0)
-        turn_x1(7)
-        quantize(("x1", 7))
-        row_norm(3)
-        b2_bank = next_bank()
-        nc.tensor.matmul(b2_bank[:, 0:H_TILES], lhsT=b2_rows[:], rhs=pick[:], start=True, stop=True)
-        nc.scalar.copy(out=b2_cols[:], in_=b2_bank[:, 0:H_TILES])
-        for t in range(4, 8):
-            product1(t)
-            add_b1(t)
-            row_norm(t)
-        mask_a(2)
+        def min_and_store(t):
+            nc.vector.tensor_tensor(out=out_sb[t][:], in0=c_sb[t][:], in1=back_bank[t][:], op=ALU.min)
+            nc.sync.dma_start(out=out_rows[:, t, :], in_=out_sb[t][:])
 
+
+        turn_x1(0)
+        interleave(("x1", 0))
+        nc.scalar.copy(out=b1_all[:], in_=spread_row(b1_row)[:])
+        rr_bank = spread_row(rr_row)
+        quantize(("x1", 0))
+        is_kept(keep_all[:], rr_bank[:])
+        for t in range(1, 4):
+            turn_x1(t)
+            interleave(("x1", t))
+            quantize(("x1", t))
+
+        for t in pair(0):
+            product1(t)
+        for t in pair(2):
+            turn_x1(t)
+        for t in pair(0):
+            add_b1(t)
+        for t in pair(2):
+            interleave(("x1", t))
+        for t in pair(0):
+            row_norm(t)
+        for t_noise, t in zip(pair(0), pair(2)):
+            mask_noise(t_noise)
+            quantize(("x1", t))
+
+        for t in pair(1):
+            product1(t)
+        col_bank = turn_col_rows()
+        for t in pair(3):
+            turn_x1(t)
+        turn_x2(1)
+        for t in pair(1):
+            add_b1(t)
+        nc.vector.tensor_copy(out=b2_cols[:], in_=col_bank[:, 0:H_TILES])
+        is_kept(keep_cols[:], col_bank[:, H_TILES : 2 * H_TILES])
+        for t in pair(3):
+            interleave(("x1", t))
+        for t in pair(1):
+            row_norm(t)
+        quantize(("x1", 6))
+        interleave(("x2", 1, 0), copy=nc.vector.tensor_copy)
+        quantize(("x1", 7))
+        interleave(("x2", 1, 1))
+
+        for t in pair(2):
+            product1(t)
+        for g, t in enumerate(pair(2)):
+            add_b1(t)
+            quantize(("x2", 1, g))
+        for t in pair(3):
+            product1(t)
+        for t in pair(3):
+            add_b1(t)
+        for t in pair(2) + pair(3):
+            row_norm(t)
+        product2(1)
+
+        turn_x2(2)
+        mask_a(0)
         nc.vector.tensor_reduce(out=extremes[:, 0:1], in_=norms[:], axis=AXIS.X, op=ALU.min)
         nc.vector.tensor_reduce(out=extremes[:, 1:2], in_=norms[:], axis=AXIS.X, op=ALU.max)
-        turn_x2(0, 0)
-        turn_x2(0, 1)
-        quantize(("x2", 0, 0))
-        mask_noise(1)
-        quantize(("x2", 0, 1))
-        turn_x2(1, 0)
-        turn_x2(1, 1)
+        mask_a(1)
         ends_bank = next_bank()
         for e in range(2):
             nc.tensor.transpose(
                 ends_bank[:, P * e : P * (e + 1)], extremes[:, e : e + 1].to_broadcast([P, P]), ident[:]
             )
-        mask_a(3)
+        turn_x2(3)
+        add_b2(1, halves=(0,))
+        for g in range(PASSES):
+            interleave(("x2", 2, g))
+        add_b2(1, halves=(1,))
+        for g in range(PASSES):
+            interleave(("x2", 3, g))
         nc.vector.tensor_reduce(out=lowest[:], in_=ends_bank[:, 0:P], axis=AXIS.X, op=ALU.min)
-        mask_noise(2)
-        spans = keep_tile("spans", [P, P], F32)
+        quantize(("x2", 2, 0))
+        above_lowest = resident("above_lowest", [P, P], F32)
         nc.vector.tensor_scalar(
-            out=spans[:],
+            out=above_lowest[:],
             in0=ends_bank[:, P : 2 * P],
             scalar1=lowest[:, 0:1],
             scalar2=None,
@@ -305,41 +376,46 @@ def tile_splitnn_pa_kernel(
             op1=ALU.max,
             accum_out=noise_mul[:],
         )
-        quantize(("x2", 1, 0))
-        mask_noise(3)
-        quantize(("x2", 1, 1))
+        quantize(("x2", 2, 1))
+
+        product2(2)
+        for t in pair(1):
+            add_noise(t)
+        for g in range(PASSES):
+            quantize(("x2", 3, g))
+        turn_x2(0)
+        turn_c(1)
+
+        product2(3)
+        add_b2(2)
+        for g in range(PASSES):
+            interleave(("x2", 0, g))
+        add_b2(3)
+        for t in pair(2):
+            add_noise(t)
+        turn_c(2)
+        mask_and_min(1)
+        for g in range(PASSES):
+            quantize(("x2", 0, g))
+        turn_back(1, outT_sb[1])
 
         product2(0)
-        for t in range(4):
+        for t in pair(1):
+            copy_and_store(t)
+        for t in pair(3):
             add_noise(t)
-        turn_x2(2, 0)
-        turn_x2(2, 1)
-        turn_back(0)
-        product2(1)
-        quantize(("x2", 2, 0))
-        quantize(("x2", 2, 1))
-        finish(0)
-        add_noise(4)
-        finish(1)
-        mask_c(4)
-        turn_x2(3, 0)
-        turn_x2(3, 1)
-        turn_back(1)
-        product2(2)
-        add_noise(5)
-        quantize(("x2", 3, 0))
-        mask_c(5)
-        quantize(("x2", 3, 1))
-        product2(3)
-        turn_back(2)
-        add_noise(6)
-        finish(2)
-        mask_c(6)
-        finish(3)
-        turn_back(3)
-        add_noise(7)
-        finish(4)
-        mask_c(7)
-        finish(5)
-        finish(6)
-        finish(7)
+        turn_c(3)
+        add_b2(0)
+        mask_and_min(2)
+        turn_back(2, outT_sb[2])
+        for t in pair(2):
+            copy_and_store(t)
+        mask_and_min(3)
+
+        turn_back(0, dT_sb[0])
+        turn_back(3, outT_sb[3])
+        for t in pair(0):
+            add_noise(t)
+        for t_copy, t_min in zip(pair(3), pair(0)):
+            copy_and_store(t_copy)
+            min_and_store(t_min)

@@ -242,15 +242,14 @@ def tile_splitnn_pa_kernel(
                         )
                 p2_bank[(j, half)] = bank
 
-        def add_b2(j, halves=(0, 1)):
-            for half in halves:
-                for h in pair(half):
-                    nc.scalar.activation(
-                        out=dT_sb[j][:, h, :],
-                        in_=p2_bank[(j, half)][:, half_cols(h)],
-                        func=ACT.Identity,
-                        bias=b2_cols[:, h : h + 1],
-                    )
+        def add_b2(j):
+            for h in range(H_TILES):
+                nc.scalar.activation(
+                    out=dT_sb[j][:, h, :],
+                    in_=p2_bank[(j, h // 2)][:, half_cols(h)],
+                    func=ACT.Identity,
+                    bias=b2_cols[:, h : h + 1],
+                )
 
         def turn_c(j):
             for half in range(2):
@@ -336,12 +335,12 @@ def tile_splitnn_pa_kernel(
 
         for t in pair(2):
             product1(t)
-        for g, t in enumerate(pair(2)):
-            add_b1(t)
+        add_b1(4)
+        for g in range(PASSES):
             quantize(("x2", 1, g))
         for t in pair(3):
             product1(t)
-        for t in pair(3):
+        for t in range(5, TILES):
             add_b1(t)
         for t in pair(2) + pair(3):
             row_norm(t)
@@ -358,14 +357,14 @@ def tile_splitnn_pa_kernel(
                 ends_bank[:, P * e : P * (e + 1)], extremes[:, e : e + 1].to_broadcast([P, P]), ident[:]
             )
         turn_x2(3)
-        add_b2(1, halves=(0,))
         for g in range(PASSES):
             interleave(("x2", 2, g))
-        add_b2(1, halves=(1,))
+        add_b2(1)
         for g in range(PASSES):
             interleave(("x2", 3, g))
-        nc.vector.tensor_reduce(out=lowest[:], in_=ends_bank[:, 0:P], axis=AXIS.X, op=ALU.min)
         quantize(("x2", 2, 0))
+        nc.vector.tensor_reduce(out=lowest[:], in_=ends_bank[:, 0:P], axis=AXIS.X, op=ALU.min)
+        quantize(("x2", 2, 1))
         above_lowest = resident("above_lowest", [P, P], F32)
         nc.vector.tensor_scalar(
             out=above_lowest[:],
@@ -376,7 +375,6 @@ def tile_splitnn_pa_kernel(
             op1=ALU.max,
             accum_out=noise_mul[:],
         )
-        quantize(("x2", 2, 1))
 
         product2(2)
         for t in pair(1):

from contextlib import ExitStack

import concourse.mybir as mybir
from concourse.masks import make_identity

B, F, H = 1024, 1024, 512
NOISE_GAIN = 30.0 / 4.0
P_KEEP = 0.95
FLOPS = 2 * 2 * B * F * H

F32 = mybir.dt.float32
BF16 = mybir.dt.bfloat16
I32 = mybir.dt.int32
U32 = mybir.dt.uint32
U8 = mybir.dt.uint8
E5M2 = mybir.dt.float8_e5m2_x4
E2M1 = mybir.dt.float4_e2m1fn_x4
ALU = mybir.AluOpType
ACT = mybir.ActivationFunctionType
AXIS = mybir.AxisListType

P = 128
TILES = B // P
PAIRS = TILES // 2
PAIR_ROWS = 2 * P
PASSES = F // 512
PASS_WORDS = 256
H_TILES = H // P
BANKS = 8
BANK_COLS = 512
OPERANDS = 2 * TILES
STAGED_BUFS = 6


def tile_splitnn_pa_kernel(
    tc, x1, x2, W1_words, W1_scales, b1, W2_words, W2_scales, b2, noise_std, rr_uniform, out
):
    nc = tc.nc
    x1_rows = x1.rearrange("(p t) k -> p t k", t=TILES)
    x2_rows = x2.rearrange("(p t) k -> p t k", t=TILES)
    noise_rows = noise_std.rearrange("(p t) h -> p t h", t=TILES)
    out_rows = out.rearrange("(p t) h -> p t h", t=TILES)

    with ExitStack() as ctx:
        sb = ctx.enter_context(tc.tile_pool(name="sb", bufs=1))
        psum = ctx.enter_context(tc.psum_pool(name="psum", bufs=1))
        ctx.enter_context(tc.manual_schedule())

        banks_taken = []

        def next_bank():
            tag = "bank%d" % (len(banks_taken) % BANKS)
            banks_taken.append(tag)
            bank = psum.tile([P, BANK_COLS], F32, name=tag, tag=tag)
            return bank

        def resident(name, shape, dtype):
            tile = sb.tile(shape, dtype, name=name, tag=name, align_bytes=64)
            return tile

        ident = resident("ident", [P, P], F32)
        pick = resident("pick", [P, 2 * H_TILES], BF16)
        b1_row = resident("b1_row", [P, H], BF16)
        rr_row = resident("rr_row", [P, H], BF16)
        col_rows = resident("col_rows", [P, P], BF16)
        b1_all = resident("b1_all", [P, H], F32)
        keep_all = resident("keep_all", [P, H], BF16)
        b2_cols = resident("b2_cols", [P, H_TILES], F32)
        keep_cols = resident("keep_cols", [P, H_TILES], F32)
        w_words = [resident("w_words%d" % c, [P, PASSES, 2 * H], U8) for c in range(2)]
        w_scales = [resident("w_scales%d" % c, [P, PASSES, H], U8) for c in range(2)]
        x1_sb = [resident("x1_sb%d" % j, [P, 2, F], BF16) for j in range(PAIRS)]
        x2_sb = [resident("x2_sb%d" % j, [P, 2, F], BF16) for j in range(PAIRS)]
        noise_sb = [resident("noise_sb%d" % j, [P, 2, H], BF16) for j in range(PAIRS)]
        norms = resident("norms", [P, TILES], F32)
        extremes = resident("extremes", [P, 2], F32)
        lowest = resident("lowest", [P, 1], F32)
        noise_mul = resident("noise_mul", [P, 1], F32)
        a_sb = [resident("a_sb%d" % t, [P, H], F32) for t in range(TILES)]
        a_kept = [resident("a_kept%d" % t, [P, H], F32) for t in range(2)]
        noise_kept = [resident("noise_kept%d" % t, [P, H], BF16) for t in range(2)]
        c_sb = [resident("c_sb%d" % t, [P, H], F32) for t in range(TILES)]
        dT_sb = [resident("dT_sb%d" % j, [P, H_TILES, PAIR_ROWS], F32) for j in range(PAIRS)]
        outT_sb = dict((j, resident("outT_sb%d" % j, [P, H_TILES, PAIR_ROWS], F32)) for j in range(1, PAIRS))
        out_sb = [resident("out_sb%d" % t, [P, H], F32) for t in range(TILES)]

        def pair(j):
            return (2 * j, 2 * j + 1)


        def load_pair(tiles, rows, j):
            nc.sync.dma_start(out=tiles[j][:], in_=rows[:, 2 * j : 2 * j + 2, :])

        def load_weights(c, words, scale_rows):
            nc.sync.dma_start(out=w_words[c][:].bitcast(I32), in_=words.rearrange("g p n -> p g n").bitcast(I32))
            for q in range(4):
                nc.sync.dma_start(
                    out=w_scales[c][32 * q : 32 * q + 4, :, :].bitcast(I32),
                    in_=scale_rows[:, 4 * q : 4 * q + 4, :].rearrange("g r n -> r g n").bitcast(I32),
                )

        make_identity(nc, ident[:])
        nc.vector.memset(b1_row[:], 0.0)
        nc.vector.memset(w_scales[0][:].bitcast(I32), 0)
        nc.vector.memset(rr_row[:], 0.0)
        nc.vector.memset(col_rows[:], 0.0)
        nc.vector.memset(w_scales[1][:].bitcast(I32), 0)
        nc.scalar.activation(out=pick[:], in_=ident[:, 0 : 2 * H_TILES], func=ACT.Identity)

        nc.sync.dma_start(out=x1_sb[0][:, 0, :], in_=x1_rows[:, 0, :])
        nc.sync.dma_start(out=b1_row[0:1, :], in_=b1.rearrange("(o n) -> o n", o=1))
        nc.sync.dma_start(out=rr_row[0:1, :], in_=rr_uniform.rearrange("(o n) -> o n", o=1))
        nc.sync.dma_start(out=x1_sb[0][:, 1, :], in_=x1_rows[:, 1, :])
        load_pair(x1_sb, x1_rows, 1)
        load_weights(0, W1_words, W1_scales)
        load_pair(x1_sb, x1_rows, 2)
        load_pair(noise_sb, noise_rows, 0)
        load_pair(x1_sb, x1_rows, 3)
        nc.sync.dma_start(out=col_rows[0:H_TILES, :], in_=b2.rearrange("(h p) -> h p", p=P))
        nc.sync.dma_start(out=col_rows[H_TILES : 2 * H_TILES, :], in_=rr_uniform.rearrange("(h p) -> h p", p=P))
        load_pair(x2_sb, x2_rows, 1)
        load_weights(1, W2_words, W2_scales)
        load_pair(x2_sb, x2_rows, 2)
        load_pair(noise_sb, noise_rows, 1)
        load_pair(x2_sb, x2_rows, 3)
        load_pair(noise_sb, noise_rows, 2)
        load_pair(noise_sb, noise_rows, 3)
        load_pair(x2_sb, x2_rows, 0)


        def spread_row(row_tile):
            bank = next_bank()
            nc.tensor.matmul(bank[:], lhsT=pick[:, 0:1].to_broadcast([P, P]), rhs=row_tile[:], start=True, stop=True)
            return bank

        def is_kept(dst, uniform):
            nc.vector.tensor_scalar(out=dst, in0=uniform, scalar1=P_KEEP, scalar2=None, op0=ALU.is_lt)

        def turn_col_rows():
            bank = next_bank()
            nc.tensor.matmul(bank[:, 0 : 2 * H_TILES], lhsT=col_rows[:], rhs=pick[:], start=True, stop=True)
            return bank


        turned, staged, codes, scales = {}, {}, {}, {}

        def turn(key, sources):
            bank = next_bank()
            for s, (rows, g) in enumerate(sources):
                words = rows.bitcast(F32)
                for u in range(2):
                    nc.tensor.transpose(
                        bank[:, P * (2 * s + u) : P * (2 * s + u + 1)],
                        words[:, PASS_WORDS * g + u : PASS_WORDS * (g + 1) : 2],
                        ident[:],
                    )
            turned[key] = bank

        def turn_x1(t):
            turn(("x1", t), [(x1_sb[t // 2][:, t % 2, :], g) for g in range(PASSES)])

        def turn_x2(j):
            for g in range(PASSES):
                turn(("x2", j, g), [(x2_sb[j][:, s, :], g) for s in range(2)])

        def interleave(key, copy=nc.scalar.copy):
            tile = sb.tile([P, 2 * BANK_COLS], BF16, name="staged", tag="staged", bufs=STAGED_BUFS, align_bytes=64)
            copy(
                out=tile[:].bitcast(F32).rearrange("p (s r u) -> p s r u", s=2, u=2),
                in_=turned[key][:].rearrange("p (s u r) -> p s r u", s=2, u=2),
            )
            staged[key] = tile

        def quantize(key):
            words = sb.tile([P, 2 * P], U32, name="codes", tag="codes", bufs=OPERANDS, align_bytes=64)
            scale_bytes = sb.tile([P, 2 * P], U8, name="scales", tag="scales", bufs=OPERANDS, align_bytes=64)
            nc.vector.quantize_mx(out=words[:].bitcast(E5M2), scales=scale_bytes[:], in_=staged[key][:])
            codes[key] = words
            scales[key] = scale_bytes


        p1_bank = {}

        def product1(t):
            bank = next_bank()
            for g in range(PASSES):
                cols = slice(P * g, P * (g + 1))
                nc.tensor.matmul_mx(
                    out=bank[:],
                    lhsT=codes[("x1", t)][:, cols].bitcast(E5M2),
                    lhsT_scale=scales[("x1", t)][:, cols],
                    rhs=w_words[0][:, g, :].bitcast(E2M1),
                    rhs_scale=w_scales[0][:, g, :],
                    start=(g == 0),
                    stop=(g == PASSES - 1),
                )
            p1_bank[t] = bank

        def add_b1(t):
            nc.vector.tensor_tensor(out=a_sb[t][:], in0=p1_bank[t][:], in1=b1_all[:], op=ALU.add)

        def row_norm(t):
            magnitudes = sb.tile([P, H], BF16, name="magnitudes", tag="magnitudes", bufs=2)
            nc.scalar.activation(
                out=magnitudes[:], in_=a_sb[t][:], func=ACT.Abs, scale=NOISE_GAIN, accum_out=norms[:, t : t + 1]
            )

        def mask_a(t):
            nc.vector.tensor_tensor(out=a_kept[t][:], in0=a_sb[t][:], in1=keep_all[:], op=ALU.mult)

        def mask_noise(t):
            nc.vector.tensor_tensor(out=noise_kept[t][:], in0=noise_sb[0][:, t, :], in1=keep_all[:], op=ALU.mult)

        def add_noise(t):
            if t in pair(0):
                noise, a = noise_kept[t][:], a_kept[t][:]
            else:
                noise, a = noise_sb[t // 2][:, t % 2, :], a_sb[t][:]
            nc.vector.scalar_tensor_tensor(
                out=c_sb[t][:], in0=noise, scalar=noise_mul[:, 0:1], in1=a, op0=ALU.mult, op1=ALU.add
            )


        p2_bank, cT_bank, back_bank = {}, {}, {}

        def half_cols(h):
            return slice(PAIR_ROWS * (h % 2), PAIR_ROWS * (h % 2 + 1))

        def product2(j):
            for half in range(2):
                bank = next_bank()
                for h in pair(half):
                    for g in range(PASSES):
                        nc.tensor.matmul_mx(
                            out=bank[:, half_cols(h)],
                            lhsT=w_words[1][:, g, 2 * P * h : 2 * P * (h + 1)].bitcast(E2M1),
                            lhsT_scale=w_scales[1][:, g, P * h : P * (h + 1)],
                            rhs=codes[("x2", j, g)][:].bitcast(E5M2),
                            rhs_scale=scales[("x2", j, g)][:],
                            start=(g == 0),
                            stop=(g == PASSES - 1),
                        )
                p2_bank[(j, half)] = bank

        def add_b2(j):
            for h in range(H_TILES):
                nc.scalar.activation(
                    out=dT_sb[j][:, h, :],
                    in_=p2_bank[(j, h // 2)][:, half_cols(h)],
                    func=ACT.Identity,
                    bias=b2_cols[:, h : h + 1],
                )

        def turn_c(j):
            for half in range(2):
                bank = next_bank()
                for h in pair(half):
                    for s in range(2):
                        first = PAIR_ROWS * (h % 2) + P * s
                        nc.tensor.transpose(
                            bank[:, first : first + P], c_sb[2 * j + s][:, P * h : P * (h + 1)], ident[:]
                        )
                cT_bank[(j, half)] = bank

        def mask_and_min(j):
            for h in range(H_TILES):
                nc.vector.scalar_tensor_tensor(
                    out=outT_sb[j][:, h, :],
                    in0=cT_bank[(j, h // 2)][:, half_cols(h)],
                    scalar=keep_cols[:, h : h + 1],
                    in1=dT_sb[j][:, h, :],
                    op0=ALU.mult,
                    op1=ALU.min,
                )

        def turn_back(j, source):
            for s in range(2):
                bank = next_bank()
                for h in range(H_TILES):
                    nc.tensor.transpose(bank[:, P * h : P * (h + 1)], source[:, h, P * s : P * (s + 1)], ident[:])
                back_bank[2 * j + s] = bank

        def copy_and_store(t):
            nc.scalar.copy(out=out_sb[t][:], in_=back_bank[t][:])
            nc.sync.dma_start(out=out_rows[:, t, :], in_=out_sb[t][:])

        def min_and_store(t):
            nc.vector.tensor_tensor(out=out_sb[t][:], in0=c_sb[t][:], in1=back_bank[t][:], op=ALU.min)
            nc.sync.dma_start(out=out_rows[:, t, :], in_=out_sb[t][:])


        turn_x1(0)
        interleave(("x1", 0))
        nc.scalar.copy(out=b1_all[:], in_=spread_row(b1_row)[:])
        rr_bank = spread_row(rr_row)
        quantize(("x1", 0))
        is_kept(keep_all[:], rr_bank[:])
        for t in range(1, 4):
            turn_x1(t)
            interleave(("x1", t))
            quantize(("x1", t))

        for t in pair(0):
            product1(t)
        for t in pair(2):
            turn_x1(t)
        for t in pair(0):
            add_b1(t)
        for t in pair(2):
            interleave(("x1", t))
        for t in pair(0):
            row_norm(t)
        for t_noise, t in zip(pair(0), pair(2)):
            mask_noise(t_noise)
            quantize(("x1", t))

        for t in pair(1):
            product1(t)
        col_bank = turn_col_rows()
        for t in pair(3):
            turn_x1(t)
        turn_x2(1)
        for t in pair(1):
            add_b1(t)
        nc.vector.tensor_copy(out=b2_cols[:], in_=col_bank[:, 0:H_TILES])
        is_kept(keep_cols[:], col_bank[:, H_TILES : 2 * H_TILES])
        for t in pair(3):
            interleave(("x1", t))
        for t in pair(1):
            row_norm(t)
        quantize(("x1", 6))
        interleave(("x2", 1, 0), copy=nc.vector.tensor_copy)
        quantize(("x1", 7))
        interleave(("x2", 1, 1))

        for t in pair(2):
            product1(t)
        add_b1(4)
        for g in range(PASSES):
            quantize(("x2", 1, g))
        for t in pair(3):
            product1(t)
        for t in range(5, TILES):
            add_b1(t)
        for t in pair(2) + pair(3):
            row_norm(t)
        product2(1)

        turn_x2(2)
        mask_a(0)
        nc.vector.tensor_reduce(out=extremes[:, 0:1], in_=norms[:], axis=AXIS.X, op=ALU.min)
        nc.vector.tensor_reduce(out=extremes[:, 1:2], in_=norms[:], axis=AXIS.X, op=ALU.max)
        mask_a(1)
        ends_bank = next_bank()
        for e in range(2):
            nc.tensor.transpose(
                ends_bank[:, P * e : P * (e + 1)], extremes[:, e : e + 1].to_broadcast([P, P]), ident[:]
            )
        turn_x2(3)
        for g in range(PASSES):
            interleave(("x2", 2, g))
        add_b2(1)
        for g in range(PASSES):
            interleave(("x2", 3, g))
        quantize(("x2", 2, 0))
        nc.vector.tensor_reduce(out=lowest[:], in_=ends_bank[:, 0:P], axis=AXIS.X, op=ALU.min)
        quantize(("x2", 2, 1))
        above_lowest = resident("above_lowest", [P, P], F32)
        nc.vector.tensor_scalar(
            out=above_lowest[:],
            in0=ends_bank[:, P : 2 * P],
            scalar1=lowest[:, 0:1],
            scalar2=None,
            op0=ALU.subtract,
            op1=ALU.max,
            accum_out=noise_mul[:],
        )

        product2(2)
        for t in pair(1):
            add_noise(t)
        for g in range(PASSES):
            quantize(("x2", 3, g))
        turn_x2(0)
        turn_c(1)

        product2(3)
        add_b2(2)
        for g in range(PASSES):
            interleave(("x2", 0, g))
        add_b2(3)
        for t in pair(2):
            add_noise(t)
        turn_c(2)
        mask_and_min(1)
        for g in range(PASSES):
            quantize(("x2", 0, g))
        turn_back(1, outT_sb[1])

        product2(0)
        for t in pair(1):
            copy_and_store(t)
        for t in pair(3):
            add_noise(t)
        turn_c(3)
        add_b2(0)
        mask_and_min(2)
        turn_back(2, outT_sb[2])
        for t in pair(2):
            copy_and_store(t)
        mask_and_min(3)

        turn_back(0, dT_sb[0])
        turn_back(3, outT_sb[3])
        for t in pair(0):
            add_noise(t)
        for t_copy, t_min in zip(pair(3), pair(0)):
            copy_and_store(t_copy)
            min_and_store(t_min)
